import numpy as np
import ml_dtypes

BF16 = ml_dtypes.bfloat16


def bf(x):
    return np.asarray(x, np.float32).astype(BF16)


def f32(x):
    return np.asarray(x, np.float32)


def f64(x):
    return np.asarray(x).astype(np.float64)


def striped(idx):
    return np.tile(idx.reshape(-1, 16).T, (8, 1))


D, S, M, N, AFZ = 128, 4096, 256, 2048, 32


def setup_inputs():
    return {"table": bf(np.random.standard_normal((D, S))), "w": bf(np.random.standard_normal((D, M)) / np.sqrt(D)), "xq": f32(np.random.standard_normal((D, N))), "offs": striped(np.random.permutation(np.tile(np.arange(S), 2))[:N])}


def reference(table, w, xq, offs):
    idx = offs[:16].T.reshape(-1)
    kv = f64(w).T @ f64(table)[:, idx]
    return np.concatenate([f64(xq) * kv[:D] / np.sqrt(AFZ), kv[D:]], axis=0)

@@ -1,0 +1,46 @@
+import math
+
+import concourse.mybir as mybir
+
+BF16, F32, U16 = mybir.dt.bfloat16, mybir.dt.float32, mybir.dt.uint16
+MULT = mybir.AluOpType.mult
+
+D = 128
+S = 4096
+N = 2048
+HEAD = 32
+PIECE = 512
+FLOPS = 2 * D * (2 * D) * N
+
+
+def tile_edgeattention_kernel(tc, table, w, xq, offs, out):
+    nc = tc.nc
+    with (
+        tc.tile_pool(name="held", bufs=1) as held,
+        tc.tile_pool(name="staged", bufs=4) as staged,
+        tc.psum_pool(name="psum", bufs=4) as psum,
+    ):
+        offsets = held.tile([D, N // 16], U16, name="offsets")
+        nc.sync.dma_start(offsets[:], offs)
+        weights = held.tile([D, 2 * D], BF16, name="weights")
+        nc.scalar.dma_start(weights[:], w)
+        stored = held.tile([D, S], BF16, name="stored")
+        nc.sync.dma_start(stored[:], table)
+        query = held.tile([D, N], F32, name="query")
+        nc.scalar.dma_start(query[:], xq)
+
+        for p in range(N // PIECE):
+            cols = slice(p * PIECE, (p + 1) * PIECE)
+            piece = offsets[:, p * PIECE // 16 : (p + 1) * PIECE // 16]
+
+            value_ps = psum.tile([D, PIECE], F32, name="value_ps")
+            nc.tensor.matmul(value_ps[:], weights[:, D : 2 * D], stored[:].indirect(piece), start=True, stop=True)
+            value_sb = staged.tile([D, PIECE], F32, name="value_sb")
+            nc.scalar.copy(value_sb[:], value_ps[:])
+            nc.scalar.dma_start(out[D : 2 * D, cols], value_sb[:])
+
+            key_ps = psum.tile([D, PIECE], F32, name="key_ps")
+            nc.tensor.matmul(key_ps[:], weights[:, 0:D], stored[:].indirect(piece), start=True, stop=True)
+            key_sb = staged.tile([D, PIECE], F32, name="key_sb")
+            nc.vector.scalar_tensor_tensor(key_sb[:], key_ps[:], 1.0 / math.sqrt(HEAD), query[:, cols], MULT, MULT)
+            nc.sync.dma_start(out[0:D, cols], key_sb[:])

@@ -20,14 +20,14 @@ def tile_edgeattention_kernel(tc, table, w, xq, offs, out):
         tc.tile_pool(name="staged", bufs=4) as staged,
         tc.psum_pool(name="psum", bufs=4) as psum,
     ):
+        stored = held.tile([D, S], BF16, name="stored")
+        nc.scalar.dma_start(stored[:], table)
+        query = held.tile([D, N], F32, name="query")
+        nc.scalar.dma_start(query[:], xq)
         offsets = held.tile([D, N // 16], U16, name="offsets")
         nc.sync.dma_start(offsets[:], offs)
         weights = held.tile([D, 2 * D], BF16, name="weights")
-        nc.scalar.dma_start(weights[:], w)
-        stored = held.tile([D, S], BF16, name="stored")
-        nc.sync.dma_start(stored[:], table)
-        query = held.tile([D, N], F32, name="query")
-        nc.scalar.dma_start(query[:], xq)
+        nc.sync.dma_start(weights[:], w)
 
         for p in range(N // PIECE):
             cols = slice(p * PIECE, (p + 1) * PIECE)

@@ -10,6 +10,7 @@ S = 4096
 N = 2048
 HEAD = 32
 PIECE = 512
+WARM = 8
 FLOPS = 2 * D * (2 * D) * N
 
 
@@ -28,6 +29,12 @@ def tile_edgeattention_kernel(tc, table, w, xq, offs, out):
         nc.sync.dma_start(offsets[:], offs)
         weights = held.tile([D, 2 * D], BF16, name="weights")
         nc.sync.dma_start(weights[:], w)
+
+        zeros = held.tile([D, PIECE], BF16, name="zeros")
+        nc.vector.memset(zeros[:], 0.0)
+        warm_ps = psum.tile([D, PIECE], F32, name="warm_ps", tag="value_ps")
+        for i in range(WARM):
+            nc.tensor.matmul(warm_ps[:], zeros[:, 0:D], zeros[:], start=True, stop=True)
 
         for p in range(N // PIECE):
             cols = slice(p * PIECE, (p + 1) * PIECE)

@@ -10,7 +10,6 @@ S = 4096
 N = 2048
 HEAD = 32
 PIECE = 512
-WARM = 8
 FLOPS = 2 * D * (2 * D) * N
 
 
@@ -30,22 +29,18 @@ def tile_edgeattention_kernel(tc, table, w, xq, offs, out):
         weights = held.tile([D, 2 * D], BF16, name="weights")
         nc.sync.dma_start(weights[:], w)
 
-        zeros = held.tile([D, PIECE], BF16, name="zeros")
-        nc.vector.memset(zeros[:], 0.0)
-        warm_ps = psum.tile([D, PIECE], F32, name="warm_ps", tag="value_ps")
-        for i in range(WARM):
-            nc.tensor.matmul(warm_ps[:], zeros[:, 0:D], zeros[:], start=True, stop=True)
-
         for p in range(N // PIECE):
             cols = slice(p * PIECE, (p + 1) * PIECE)
             piece = offsets[:, p * PIECE // 16 : (p + 1) * PIECE // 16]
-
             value_ps = psum.tile([D, PIECE], F32, name="value_ps")
             nc.tensor.matmul(value_ps[:], weights[:, D : 2 * D], stored[:].indirect(piece), start=True, stop=True)
             value_sb = staged.tile([D, PIECE], F32, name="value_sb")
             nc.scalar.copy(value_sb[:], value_ps[:])
             nc.scalar.dma_start(out[D : 2 * D, cols], value_sb[:])
 
+        for p in range(N // PIECE):
+            cols = slice(p * PIECE, (p + 1) * PIECE)
+            piece = offsets[:, p * PIECE // 16 : (p + 1) * PIECE // 16]
             key_ps = psum.tile([D, PIECE], F32, name="key_ps")
             nc.tensor.matmul(key_ps[:], weights[:, 0:D], stored[:].indirect(piece), start=True, stop=True)
             key_sb = staged.tile([D, PIECE], F32, name="key_sb")

@@ -10,6 +10,7 @@ S = 4096
 N = 2048
 HEAD = 32
 PIECE = 512
+STORE = 1024
 FLOPS = 2 * D * (2 * D) * N
 
 
@@ -17,7 +18,7 @@ def tile_edgeattention_kernel(tc, table, w, xq, offs, out):
     nc = tc.nc
     with (
         tc.tile_pool(name="held", bufs=1) as held,
-        tc.tile_pool(name="staged", bufs=4) as staged,
+        tc.tile_pool(name="staged", bufs=2) as staged,
         tc.psum_pool(name="psum", bufs=4) as psum,
     ):
         stored = held.tile([D, S], BF16, name="stored")
@@ -29,20 +30,24 @@ def tile_edgeattention_kernel(tc, table, w, xq, offs, out):
         weights = held.tile([D, 2 * D], BF16, name="weights")
         nc.sync.dma_start(weights[:], w)
 
-        for p in range(N // PIECE):
-            cols = slice(p * PIECE, (p + 1) * PIECE)
-            piece = offsets[:, p * PIECE // 16 : (p + 1) * PIECE // 16]
-            value_ps = psum.tile([D, PIECE], F32, name="value_ps")
-            nc.tensor.matmul(value_ps[:], weights[:, D : 2 * D], stored[:].indirect(piece), start=True, stop=True)
-            value_sb = staged.tile([D, PIECE], F32, name="value_sb")
-            nc.scalar.copy(value_sb[:], value_ps[:])
-            nc.scalar.dma_start(out[D : 2 * D, cols], value_sb[:])
+        for s in range(N // STORE):
+            value_sb = staged.tile([D, STORE], F32, name="value_sb")
+            for c in range(0, STORE, PIECE):
+                first = s * STORE + c
+                piece = offsets[:, first // 16 : (first + PIECE) // 16]
+                value_ps = psum.tile([D, PIECE], F32, name="value_ps")
+                nc.tensor.matmul(value_ps[:], weights[:, D : 2 * D], stored[:].indirect(piece), start=True, stop=True)
+                nc.scalar.copy(value_sb[:, c : c + PIECE], value_ps[:])
+            nc.scalar.dma_start(out[D : 2 * D, s * STORE : (s + 1) * STORE], value_sb[:])
 
-        for p in range(N // PIECE):
-            cols = slice(p * PIECE, (p + 1) * PIECE)
-            piece = offsets[:, p * PIECE // 16 : (p + 1) * PIECE // 16]
-            key_ps = psum.tile([D, PIECE], F32, name="key_ps")
-            nc.tensor.matmul(key_ps[:], weights[:, 0:D], stored[:].indirect(piece), start=True, stop=True)
-            key_sb = staged.tile([D, PIECE], F32, name="key_sb")
-            nc.vector.scalar_tensor_tensor(key_sb[:], key_ps[:], 1.0 / math.sqrt(HEAD), query[:, cols], MULT, MULT)
-            nc.sync.dma_start(out[0:D, cols], key_sb[:])
+        for s in range(N // STORE):
+            key_sb = staged.tile([D, STORE], F32, name="key_sb")
+            for c in range(0, STORE, PIECE):
+                first = s * STORE + c
+                piece = offsets[:, first // 16 : (first + PIECE) // 16]
+                key_ps = psum.tile([D, PIECE], F32, name="key_ps")
+                nc.tensor.matmul(key_ps[:], weights[:, 0:D], stored[:].indirect(piece), start=True, stop=True)
+                nc.vector.scalar_tensor_tensor(
+                    key_sb[:, c : c + PIECE], key_ps[:], 1.0 / math.sqrt(HEAD), query[:, first : first + PIECE], MULT, MULT
+                )
+            nc.sync.dma_start(out[0:D, s * STORE : (s + 1) * STORE], key_sb[:])

@@ -18,7 +18,7 @@ def tile_edgeattention_kernel(tc, table, w, xq, offs, out):
     nc = tc.nc
     with (
         tc.tile_pool(name="held", bufs=1) as held,
-        tc.tile_pool(name="staged", bufs=2) as staged,
+        tc.tile_pool(name="staged", bufs=4) as staged,
         tc.psum_pool(name="psum", bufs=4) as psum,
     ):
         stored = held.tile([D, S], BF16, name="stored")
@@ -30,15 +30,13 @@ def tile_edgeattention_kernel(tc, table, w, xq, offs, out):
         weights = held.tile([D, 2 * D], BF16, name="weights")
         nc.sync.dma_start(weights[:], w)
 
-        for s in range(N // STORE):
-            value_sb = staged.tile([D, STORE], F32, name="value_sb")
-            for c in range(0, STORE, PIECE):
-                first = s * STORE + c
-                piece = offsets[:, first // 16 : (first + PIECE) // 16]
-                value_ps = psum.tile([D, PIECE], F32, name="value_ps")
-                nc.tensor.matmul(value_ps[:], weights[:, D : 2 * D], stored[:].indirect(piece), start=True, stop=True)
-                nc.scalar.copy(value_sb[:, c : c + PIECE], value_ps[:])
-            nc.scalar.dma_start(out[D : 2 * D, s * STORE : (s + 1) * STORE], value_sb[:])
+        for first in range(0, N, PIECE):
+            piece = offsets[:, first // 16 : (first + PIECE) // 16]
+            value_ps = psum.tile([D, PIECE], F32, name="value_ps")
+            nc.tensor.matmul(value_ps[:], weights[:, D : 2 * D], stored[:].indirect(piece), start=True, stop=True)
+            value_sb = staged.tile([D, PIECE], F32, name="value_sb")
+            nc.scalar.copy(value_sb[:], value_ps[:])
+            nc.scalar.dma_start(out[D : 2 * D, first : first + PIECE], value_sb[:])
 
         for s in range(N // STORE):
             key_sb = staged.tile([D, STORE], F32, name="key_sb")

import math

import concourse.mybir as mybir

BF16, F32, U16 = mybir.dt.bfloat16, mybir.dt.float32, mybir.dt.uint16
MULT = mybir.AluOpType.mult

D = 128
S = 4096
N = 2048
HEAD = 32
PIECE = 512
STORE = 1024
FLOPS = 2 * D * (2 * D) * N


def tile_edgeattention_kernel(tc, table, w, xq, offs, out):
    nc = tc.nc
    with (
        tc.tile_pool(name="held", bufs=1) as held,
        tc.tile_pool(name="staged", bufs=4) as staged,
        tc.psum_pool(name="psum", bufs=4) as psum,
    ):
        stored = held.tile([D, S], BF16, name="stored")
        nc.scalar.dma_start(stored[:], table)
        query = held.tile([D, N], F32, name="query")
        nc.scalar.dma_start(query[:], xq)
        offsets = held.tile([D, N // 16], U16, name="offsets")
        nc.sync.dma_start(offsets[:], offs)
        weights = held.tile([D, 2 * D], BF16, name="weights")
        nc.sync.dma_start(weights[:], w)

        for first in range(0, N, PIECE):
            piece = offsets[:, first // 16 : (first + PIECE) // 16]
            value_ps = psum.tile([D, PIECE], F32, name="value_ps")
            nc.tensor.matmul(value_ps[:], weights[:, D : 2 * D], stored[:].indirect(piece), start=True, stop=True)
            value_sb = staged.tile([D, PIECE], F32, name="value_sb")
            nc.scalar.copy(value_sb[:], value_ps[:])
            nc.scalar.dma_start(out[D : 2 * D, first : first + PIECE], value_sb[:])

        for s in range(N // STORE):
            key_sb = staged.tile([D, STORE], F32, name="key_sb")
            for c in range(0, STORE, PIECE):
                first = s * STORE + c
                piece = offsets[:, first // 16 : (first + PIECE) // 16]
                key_ps = psum.tile([D, PIECE], F32, name="key_ps")
                nc.tensor.matmul(key_ps[:], weights[:, 0:D], stored[:].indirect(piece), start=True, stop=True)
                nc.vector.scalar_tensor_tensor(
                    key_sb[:, c : c + PIECE], key_ps[:], 1.0 / math.sqrt(HEAD), query[:, first : first + PIECE], MULT, MULT
                )
            nc.sync.dma_start(out[0:D, s * STORE : (s + 1) * STORE], key_sb[:])
